import numpy as np
import ml_dtypes


def mxq(x, axis, fmt="e4m3"):
    dtype, down = {"e4m3": (ml_dtypes.float8_e4m3fn, 7), "e5m2": (ml_dtypes.float8_e5m2, 14)}[fmt]
    v = np.moveaxis(np.asarray(x, np.float32).astype(ml_dtypes.bfloat16).astype(np.float64), axis, -1)
    blocks = v.reshape(v.shape[:-1] + (-1, 32))
    amax = np.abs(blocks).max(-1, keepdims=True)
    byte = np.maximum(np.where(amax > 0, np.frexp(amax)[1] - 1 + 127, 0) - down, 1)
    scale = np.exp2(byte - 127.0)
    codes = (blocks / scale).astype(np.float32).astype(dtype).astype(np.float64)
    return np.moveaxis((codes * scale).reshape(v.shape), -1, axis)


WIDE = False


def mx_kscale(k):
    if not WIDE:
        return np.ones(k)
    levels = np.array([10, -10, 5, -5, 0])
    a = np.random.permutation(np.resize(levels, k // 512 * 4)).reshape(k // 512, 4)
    idx = np.arange(k)
    return np.exp2(a[idx // 512, idx % 128 // 32])


BF16 = ml_dtypes.bfloat16


def bf(x):
    return np.asarray(x, np.float32).astype(BF16)


def f64(x):
    return np.asarray(x).astype(np.float64)


E2M1 = np.array([0.0, 0.5, 1.0, 1.5, 2.0, 3.0, 4.0, 6.0, -0.0, -0.5, -1.0, -1.5, -2.0, -3.0, -4.0, -6.0])


def pack_weight(w, fmt):
    k, n = w.shape
    w = f64(bf(w)).reshape(k // 32, 32, n)
    amax = np.abs(w).max(1)
    if fmt == "e4m3":
        byte = np.frexp(amax)[1] - 1 + 127 - 7
    else:
        mant, ex = np.frexp(amax / 6.0)
        byte = np.where(mant > 0.5, ex, ex - 1) + 127
    byte = np.clip(np.where(amax > 0, byte, 1), 1, 254)
    scaled = (w * np.exp2(127.0 - byte)[:, None, :]).reshape(k, n).astype(np.float32)
    by_word = np.ascontiguousarray(scaled.reshape(k // 512, 128, 4, n).transpose(0, 1, 3, 2))
    if fmt == "e4m3":
        words = by_word.astype(ml_dtypes.float8_e4m3fn).view(np.uint8)
    else:
        c = by_word.astype(ml_dtypes.float4_e2m1fn).view(np.uint8) & 0xF
        words = c[..., 0::2] | (c[..., 1::2] << 4)
    return np.ascontiguousarray(words), np.ascontiguousarray(byte.astype(np.uint8).reshape(k // 512, 16, n))


def unpack_weight(words, scales, fmt):
    g, p, n, _ = words.shape
    if fmt == "e4m3":
        vals = np.ascontiguousarray(words).view(ml_dtypes.float8_e4m3fn).astype(np.float64)
    else:
        nib = np.empty((g, p, n, 4), np.uint8)
        nib[..., 0::2] = words & 0xF
        nib[..., 1::2] = words >> 4
        vals = E2M1[nib]
    vals = vals * np.repeat(np.exp2(scales.astype(np.float64) - 127.0), 8, axis=1)[..., None]
    return vals.transpose(0, 1, 3, 2).reshape(g * 512, n)


B, L, C, K = 128, 8, 512, 5
F = C
BN_EPS = 1e-3
LEAKY_ALPHA = 0.3


def leaky(v):
    return np.where(v >= 0, v, LEAKY_ALPHA * v)


def bn(v, gamma, beta, mean, var):
    return gamma * (v - mean) * (1.0 / np.sqrt(var + BN_EPS)) + beta


def setup_inputs():
    s = mx_kscale(F)
    h = bf(leaky(np.random.standard_normal((B, L, F)) * 1.2) * s)
    x = bf(np.random.standard_normal((B, L, C)))
    k2 = np.random.standard_normal((K, L, F, F)) * 0.16 / np.sqrt(K * F) / s[:, None]
    k2_words, k2_scales = pack_weight(k2.reshape(-1, F), "e4m3")
    return {"h": h,
            "x": x,
            "k2_words": k2_words,
            "k2_scales": k2_scales,
            "b2": bf(np.random.standard_normal((L, F)) * 0.03),
            "gamma2": bf(1.0 + 0.1 * np.random.standard_normal(F)),
            "beta2": bf(np.random.standard_normal(F) * 0.2),
            "mean2": bf(np.random.standard_normal(F) * 0.05),
            "var2": bf(np.random.uniform(0.01, 0.03, F))}


def reference(h, x, k2_words, k2_scales, b2, gamma2, beta2, mean2, var2):
    hq = mxq(f64(h).transpose(1, 0, 2), 2, "e4m3")
    k = unpack_weight(k2_words, k2_scales, "e4m3").reshape(K, L, F, F)
    out = 2.0 * f64(b2)
    for i in range(k.shape[0]):
        step = (i // 2) * (-1 if i % 2 == 1 else 1)
        ki = k[i][(np.arange(L) + step) % L] if step != 0 else k[i]
        p = hq @ ki
        p = np.roll(p, step, axis=0) if step != 0 else p
        out = out + p.transpose(1, 0, 2)
    return leaky(bn(out, f64(gamma2), f64(beta2), f64(mean2), f64(var2)) + f64(x))

@@ -1,0 +1,183 @@
+from contextlib import ExitStack
+
+import concourse.mybir as mybir
+from concourse.masks import make_identity
+
+F32 = mybir.dt.float32
+BF16 = mybir.dt.bfloat16
+I32 = mybir.dt.int32
+U32 = mybir.dt.uint32
+U8 = mybir.dt.uint8
+FP8X4 = mybir.dt.float8_e4m3fn_x4
+ALU = mybir.AluOpType
+
+P = 128
+L = 8
+C = 512
+TAPS = 5
+TAP_STEP = (0, 0, 1, -1, 2)
+BN_EPS = 1e-3
+LEAKY_ALPHA = 0.3
+
+PACK = 4
+OFFSETS = 4
+SLOTS = TAPS * L // OFFSETS
+CHUNKS = C // P
+GAIN = L
+
+FLOPS = 2 * P * L * TAPS * C * C
+
+
+def tile_residualblock5_pb_e_kernel(tc, h, x, k2_words, k2_scales, b2, gamma2, beta2, mean2, var2, out):
+    nc = tc.nc
+    with ExitStack() as ctx:
+        keep = ctx.enter_context(tc.tile_pool(name="keep", bufs=1))
+        work = ctx.enter_context(tc.tile_pool(name="work", bufs=3))
+        psum = ctx.enter_context(tc.psum_pool(name="psum", bufs=8))
+
+        position_order = [j + OFFSETS * half for j in range(OFFSETS) for half in range(L // OFFSETS)]
+
+        ident_f32 = keep.tile([P, P], F32)
+        make_identity(nc, ident_f32[:])
+        ident_bf16 = keep.tile([P, P], BF16)
+        nc.vector.tensor_copy(out=ident_bf16[:], in_=ident_f32[:])
+
+        rows = keep.tile([P, C], BF16)
+        nc.vector.memset(rows[:], 0.0)
+        w_planes = keep.tile([P, SLOTS, C], U8, align_bytes=64)
+        nc.vector.memset(w_planes[:].rearrange("p s n -> p (s n)").bitcast(I32), 0)
+
+        nc.scalar.dma_start(out=rows[0:L, :], in_=b2)
+        for r, vec in enumerate((gamma2, beta2, mean2, var2)):
+            nc.scalar.dma_start(out=rows[L + r : L + r + 1, :], in_=vec.rearrange("(o f) -> o f", o=1))
+
+        scales_by_offset = k2_scales.rearrange("(s j) q n -> j q s n", j=OFFSETS)
+        for j in range(OFFSETS):
+            for r in range(4):
+                nc.gpsimd.dma_start(
+                    out=w_planes[4 * j + r : P : 32, :, :].bitcast(F32),
+                    in_=scales_by_offset[j, r : 16 : 4, :, :].bitcast(F32),
+                )
+
+        h_sb = keep.tile([P, L, C], BF16)
+        x_sb = keep.tile([P, L, C], BF16)
+        w_words = keep.tile([P, L, TAPS, C], U32, align_bytes=64)
+        words_by_position = k2_words.rearrange("(i l) p n t -> l p i (n t)", l=L).bitcast(I32)
+
+        def load_weights(l):
+            nc.sync.dma_start(out=w_words[:, l, :, :].bitcast(I32), in_=words_by_position[l])
+
+        half_l = L // 2
+        nc.sync.dma_start(out=h_sb[:, 0:half_l, :], in_=h[:, 0:half_l, :])
+        nc.sync.dma_start(out=h_sb[:, half_l:L, :], in_=h[:, half_l:L, :])
+        load_weights(position_order[0])
+        nc.sync.dma_start(out=x_sb[:], in_=x)
+        for l in position_order[1:]:
+            load_weights(l)
+
+        h_pairs = h_sb[:].rearrange("p l c -> p (l c)").bitcast(F32)
+        pairs = C // 2
+        grouped = keep.tile([P, L * P * PACK], BF16, align_bytes=64)
+        grouped_pairs = grouped[:].bitcast(F32).rearrange("p (l b u) -> p l b u", l=L, u=2)
+        h_codes = keep.tile([P, L * P], U32, align_bytes=64)
+        h_plane = keep.tile([P, L * P], U8, align_bytes=64)
+
+        banks_of_h = L // 2
+        for g in range(banks_of_h):
+            flipped = psum.tile([P, 2, 2, P], F32, tag="bank")
+            for l2 in range(2):
+                for u in range(2):
+                    first = (2 * g + l2) * pairs
+                    nc.tensor.transpose(
+                        flipped[:, l2, u, :], h_pairs[:, first + u : first + pairs : 2], ident_f32[:]
+                    )
+            copy_out = nc.vector.tensor_copy if g % 2 == 0 else nc.scalar.copy
+            copy_out(
+                out=grouped_pairs[:, 2 * g : 2 * g + 2, :, :], in_=flipped[:].rearrange("p l u b -> p l b u")
+            )
+        for g in range(banks_of_h):
+            cols = slice(2 * g * P, (2 * g + 2) * P)
+            nc.vector.quantize_mx(
+                out=h_codes[:, cols].bitcast(FP8X4),
+                scales=h_plane[:, cols],
+                in_=grouped[:, 2 * g * P * PACK : (2 * g + 2) * P * PACK],
+            )
+
+        rows_t_ps = psum.tile([P, CHUNKS, P], BF16, tag="bank")
+        for c in range(CHUNKS):
+            nc.tensor.transpose(rows_t_ps[:, c, :], rows[:, c * P : (c + 1) * P], ident_bf16[:])
+        rows_t = keep.tile([P, CHUNKS, L + 4], F32)
+        nc.vector.tensor_copy(out=rows_t[:], in_=rows_t_ps[:, :, 0 : L + 4])
+        b2_t = rows_t[:, :, 0:L]
+        gamma_t = rows_t[:, :, L : L + 1]
+        beta_t = rows_t[:, :, L + 1 : L + 2]
+        mean_t = rows_t[:, :, L + 2 : L + 3]
+        var_t = rows_t[:, :, L + 3 : L + 4]
+
+        std_t = keep.tile([P, CHUNKS, 1], F32)
+        rstd_t = keep.tile([P, CHUNKS, 1], F32)
+        base_t = keep.tile([P, CHUNKS, 1], F32)
+        table_t = keep.tile([P, CHUNKS, L + 1], F32)
+        gain_t = table_t[:, :, GAIN : GAIN + 1]
+        shift_t = table_t[:, :, 0:L]
+        nc.vector.tensor_scalar_add(out=std_t[:], in0=var_t, scalar1=BN_EPS)
+        nc.scalar.sqrt(out=std_t[:], in_=std_t[:])
+        nc.vector.reciprocal(out=rstd_t[:], in_=std_t[:])
+        nc.vector.tensor_mul(out=gain_t, in0=gamma_t, in1=rstd_t[:])
+        nc.vector.tensor_mul(out=base_t[:], in0=mean_t, in1=gain_t)
+        nc.vector.tensor_sub(out=base_t[:], in0=beta_t, in1=base_t[:])
+        nc.vector.scalar_tensor_tensor(
+            out=shift_t, in0=b2_t, scalar=2.0, in1=gain_t.to_broadcast([P, CHUNKS, L]), op0=ALU.mult, op1=ALU.mult
+        )
+        nc.vector.tensor_add(out=shift_t, in0=shift_t, in1=base_t[:].to_broadcast([P, CHUNKS, L]))
+
+        def spread_over_batch(column):
+            bank = psum.tile([P, C], F32, tag="bank")
+            for c in range(CHUNKS):
+                nc.tensor.matmul(
+                    out=bank[:, c * P : (c + 1) * P],
+                    lhsT=table_t[:, c, column : column + 1].to_broadcast([P, P]),
+                    rhs=ident_f32[:],
+                    start=True,
+                    stop=True,
+                )
+            return bank
+
+        gain = keep.tile([P, C], F32)
+        nc.scalar.copy(out=gain[:], in_=spread_over_batch(GAIN)[:])
+
+        addend = keep.tile([P, L, C], F32)
+        result = keep.tile([P, L, C], F32)
+
+        def prepare_addend(l):
+            nc.vector.tensor_tensor(
+                out=addend[:, l, :], in0=spread_over_batch(l)[:], in1=x_sb[:, l, :], op=ALU.add
+            )
+
+        def position(l):
+            j, half = l % OFFSETS, l // OFFSETS
+            y = psum.tile([P, C], F32, tag="bank")
+            for i in range(TAPS):
+                source = (l - TAP_STEP[i]) % L
+                nc.tensor.matmul_mx(
+                    out=y[:],
+                    lhsT=h_codes[:, source * P : (source + 1) * P].bitcast(FP8X4),
+                    lhsT_scale=h_plane[:, source * P : (source + 1) * P],
+                    rhs=w_words[:, l, i, :].bitcast(FP8X4),
+                    rhs_scale=w_planes[4 * j : P, 2 * i + half, :],
+                    start=(i == 0),
+                    stop=(i == TAPS - 1),
+                )
+            z = work.tile([P, C], F32)
+            nc.vector.tensor_tensor(out=z[:], in0=y[:], in1=gain[:], op=ALU.mult)
+            nc.vector.tensor_tensor(out=z[:], in0=z[:], in1=addend[:, l, :], op=ALU.add)
+            nc.vector.scalar_tensor_tensor(
+                out=result[:, l, :], in0=z[:], scalar=LEAKY_ALPHA, in1=z[:], op0=ALU.mult, op1=ALU.max
+            )
+            nc.scalar.dma_start(out=out[:, l, :], in_=result[:, l, :])
+
+        prepare_addend(position_order[0])
+        for n, l in enumerate(position_order):
+            if n + 1 < L:
+                prepare_addend(position_order[n + 1])
+            position(l)

@@ -62,10 +62,11 @@ def tile_residualblock5_pb_e_kernel(tc, h, x, k2_words, k2_scales, b2, gamma2, b
         h_sb = keep.tile([P, L, C], BF16)
         x_sb = keep.tile([P, L, C], BF16)
         w_words = keep.tile([P, L, TAPS, C], U32, align_bytes=64)
-        words_by_position = k2_words.rearrange("(i l) p n t -> l p i (n t)", l=L).bitcast(I32)
+        words_by_matrix = k2_words.rearrange("e p n t -> e p (n t)").bitcast(I32)
 
         def load_weights(l):
-            nc.sync.dma_start(out=w_words[:, l, :, :].bitcast(I32), in_=words_by_position[l])
+            for i in range(TAPS):
+                nc.sync.dma_start(out=w_words[:, l, i, :].bitcast(I32), in_=words_by_matrix[L * i + l])
 
         half_l = L // 2
         nc.sync.dma_start(out=h_sb[:, 0:half_l, :], in_=h[:, 0:half_l, :])

@@ -51,14 +51,6 @@ def tile_residualblock5_pb_e_kernel(tc, h, x, k2_words, k2_scales, b2, gamma2, b
         for r, vec in enumerate((gamma2, beta2, mean2, var2)):
             nc.scalar.dma_start(out=rows[L + r : L + r + 1, :], in_=vec.rearrange("(o f) -> o f", o=1))
 
-        scales_by_offset = k2_scales.rearrange("(s j) q n -> j q s n", j=OFFSETS)
-        for j in range(OFFSETS):
-            for r in range(4):
-                nc.gpsimd.dma_start(
-                    out=w_planes[4 * j + r : P : 32, :, :].bitcast(F32),
-                    in_=scales_by_offset[j, r : 16 : 4, :, :].bitcast(F32),
-                )
-
         h_sb = keep.tile([P, L, C], BF16)
         x_sb = keep.tile([P, L, C], BF16)
         w_words = keep.tile([P, L, TAPS, C], U32, align_bytes=64)
@@ -71,6 +63,15 @@ def tile_residualblock5_pb_e_kernel(tc, h, x, k2_words, k2_scales, b2, gamma2, b
         half_l = L // 2
         nc.sync.dma_start(out=h_sb[:, 0:half_l, :], in_=h[:, 0:half_l, :])
         nc.sync.dma_start(out=h_sb[:, half_l:L, :], in_=h[:, half_l:L, :])
+
+        scales_by_offset = k2_scales.rearrange("(s j) q n -> j q s n", j=OFFSETS)
+        for j in range(OFFSETS):
+            for r in range(4):
+                nc.sync.dma_start(
+                    out=w_planes[4 * j + r : P : 32, :, :].bitcast(I32),
+                    in_=scales_by_offset[j, r : 16 : 4, :, :].bitcast(I32),
+                )
+
         load_weights(position_order[0])
         nc.sync.dma_start(out=x_sb[:], in_=x)
         for l in position_order[1:]:

@@ -35,8 +35,6 @@ def tile_residualblock5_pb_e_kernel(tc, h, x, k2_words, k2_scales, b2, gamma2, b
         work = ctx.enter_context(tc.tile_pool(name="work", bufs=3))
         psum = ctx.enter_context(tc.psum_pool(name="psum", bufs=8))
 
-        position_order = [j + OFFSETS * half for j in range(OFFSETS) for half in range(L // OFFSETS)]
-
         ident_f32 = keep.tile([P, P], F32)
         make_identity(nc, ident_f32[:])
         ident_bf16 = keep.tile([P, P], BF16)
@@ -64,17 +62,17 @@ def tile_residualblock5_pb_e_kernel(tc, h, x, k2_words, k2_scales, b2, gamma2, b
         nc.sync.dma_start(out=h_sb[:, 0:half_l, :], in_=h[:, 0:half_l, :])
         nc.sync.dma_start(out=h_sb[:, half_l:L, :], in_=h[:, half_l:L, :])
 
-        scales_by_offset = k2_scales.rearrange("(s j) q n -> j q s n", j=OFFSETS)
-        for j in range(OFFSETS):
-            for r in range(4):
-                nc.sync.dma_start(
-                    out=w_planes[4 * j + r : P : 32, :, :].bitcast(I32),
-                    in_=scales_by_offset[j, r : 16 : 4, :, :].bitcast(I32),
-                )
+        scales_by_row = k2_scales.rearrange("(s j) q n -> q j s n", j=OFFSETS)
+        for q in range(16):
+            first = 32 * (q // 4) + q % 4
+            nc.sync.dma_start(
+                out=w_planes[first : first + 4 * OFFSETS : 4, :, :].bitcast(I32),
+                in_=scales_by_row[q].bitcast(I32),
+            )
 
-        load_weights(position_order[0])
+        load_weights(0)
         nc.sync.dma_start(out=x_sb[:], in_=x)
-        for l in position_order[1:]:
+        for l in range(1, L):
             load_weights(l)
 
         h_pairs = h_sb[:].rearrange("p l c -> p (l c)").bitcast(F32)
@@ -178,8 +176,8 @@ def tile_residualblock5_pb_e_kernel(tc, h, x, k2_words, k2_scales, b2, gamma2, b
             )
             nc.scalar.dma_start(out=out[:, l, :], in_=result[:, l, :])
 
-        prepare_addend(position_order[0])
-        for n, l in enumerate(position_order):
-            if n + 1 < L:
-                prepare_addend(position_order[n + 1])
+        prepare_addend(0)
+        for l in range(L):
+            if l + 1 < L:
+                prepare_addend(l + 1)
             position(l)

@@ -20,10 +20,14 @@ BN_EPS = 1e-3
 LEAKY_ALPHA = 0.3
 
 PACK = 4
+SCALE_ROWS = C // 32
 OFFSETS = 4
 SLOTS = TAPS * L // OFFSETS
 CHUNKS = C // P
+VECTORS = L + 4
 GAIN = L
+TABLE = L + 1
+TERMS = 3
 
 FLOPS = 2 * P * L * TAPS * C * C
 
@@ -39,11 +43,16 @@ def tile_residualblock5_pb_e_kernel(tc, h, x, k2_words, k2_scales, b2, gamma2, b
         make_identity(nc, ident_f32[:])
         ident_bf16 = keep.tile([P, P], BF16)
         nc.vector.tensor_copy(out=ident_bf16[:], in_=ident_f32[:])
+        pick = keep.tile([P, TABLE], BF16)
+        nc.vector.tensor_add(out=pick[:], in0=ident_bf16[:, 0:TABLE], in1=ident_bf16[:, TABLE : 2 * TABLE])
+        nc.vector.tensor_add(out=pick[:], in0=pick[:], in1=ident_bf16[:, 2 * TABLE : 3 * TABLE])
 
         rows = keep.tile([P, C], BF16)
         nc.vector.memset(rows[:], 0.0)
         w_planes = keep.tile([P, SLOTS, C], U8, align_bytes=64)
         nc.vector.memset(w_planes[:].rearrange("p s n -> p (s n)").bitcast(I32), 0)
+        terms_t = keep.tile([P, CHUNKS, P], BF16)
+        nc.vector.memset(terms_t[:], 0.0)
 
         nc.scalar.dma_start(out=rows[0:L, :], in_=b2)
         for r, vec in enumerate((gamma2, beta2, mean2, var2)):
@@ -52,28 +61,78 @@ def tile_residualblock5_pb_e_kernel(tc, h, x, k2_words, k2_scales, b2, gamma2, b
         h_sb = keep.tile([P, L, C], BF16)
         x_sb = keep.tile([P, L, C], BF16)
         w_words = keep.tile([P, L, TAPS, C], U32, align_bytes=64)
-        words_by_matrix = k2_words.rearrange("e p n t -> e p (n t)").bitcast(I32)
-
-        def load_weights(l):
-            for i in range(TAPS):
-                nc.sync.dma_start(out=w_words[:, l, i, :].bitcast(I32), in_=words_by_matrix[L * i + l])
 
         half_l = L // 2
         nc.sync.dma_start(out=h_sb[:, 0:half_l, :], in_=h[:, 0:half_l, :])
         nc.sync.dma_start(out=h_sb[:, half_l:L, :], in_=h[:, half_l:L, :])
 
         scales_by_row = k2_scales.rearrange("(s j) q n -> q j s n", j=OFFSETS)
-        for q in range(16):
+        for q in range(SCALE_ROWS):
             first = 32 * (q // 4) + q % 4
             nc.sync.dma_start(
                 out=w_planes[first : first + 4 * OFFSETS : 4, :, :].bitcast(I32),
                 in_=scales_by_row[q].bitcast(I32),
             )
 
-        load_weights(0)
         nc.sync.dma_start(out=x_sb[:], in_=x)
-        for l in range(1, L):
-            load_weights(l)
+
+        words_by_matrix = k2_words.rearrange("e p n t -> e p (n t)").bitcast(I32)
+        for l in range(L):
+            for i in range(TAPS):
+                nc.sync.dma_start(out=w_words[:, l, i, :].bitcast(I32), in_=words_by_matrix[L * i + l])
+
+        rows_t_ps = psum.tile([P, CHUNKS, P], BF16, tag="bank")
+        for c in range(CHUNKS):
+            nc.tensor.transpose(rows_t_ps[:, c, :], rows[:, c * P : (c + 1) * P], ident_bf16[:])
+        rows_t = keep.tile([P, CHUNKS, VECTORS], F32)
+        nc.vector.tensor_copy(out=rows_t[:], in_=rows_t_ps[:, :, 0:VECTORS])
+        b2_t = rows_t[:, :, 0:L]
+        gamma_t = rows_t[:, :, L : L + 1]
+        beta_t = rows_t[:, :, L + 1 : L + 2]
+        mean_t = rows_t[:, :, L + 2 : L + 3]
+        var_t = rows_t[:, :, L + 3 : L + 4]
+
+        std_t = keep.tile([P, CHUNKS, 1], F32)
+        rstd_t = keep.tile([P, CHUNKS, 1], F32)
+        base_t = keep.tile([P, CHUNKS, 1], F32)
+        table_t = keep.tile([P, CHUNKS, TABLE], F32)
+        gain_t = table_t[:, :, GAIN : GAIN + 1]
+        shift_t = table_t[:, :, 0:L]
+        nc.vector.tensor_scalar_add(out=std_t[:], in0=var_t, scalar1=BN_EPS)
+        nc.scalar.sqrt(out=std_t[:], in_=std_t[:])
+        nc.vector.reciprocal(out=rstd_t[:], in_=std_t[:])
+        nc.vector.tensor_mul(out=gain_t, in0=gamma_t, in1=rstd_t[:])
+        nc.vector.tensor_mul(out=base_t[:], in0=mean_t, in1=gain_t)
+        nc.vector.tensor_sub(out=base_t[:], in0=beta_t, in1=base_t[:])
+        nc.vector.scalar_tensor_tensor(
+            out=shift_t, in0=b2_t, scalar=2.0, in1=gain_t.to_broadcast([P, CHUNKS, L]), op0=ALU.mult, op1=ALU.mult
+        )
+        nc.vector.tensor_add(out=shift_t, in0=shift_t, in1=base_t[:].to_broadcast([P, CHUNKS, L]))
+
+        for s in range(TERMS):
+            term = terms_t[:, :, TABLE * s : TABLE * (s + 1)]
+            nc.vector.tensor_copy(out=term, in_=table_t[:])
+            if s + 1 < TERMS:
+                nc.vector.tensor_sub(out=table_t[:], in0=table_t[:], in1=term)
+        terms_ps = psum.tile([P, CHUNKS, P], BF16, tag="bank")
+        for c in range(CHUNKS):
+            nc.tensor.transpose(terms_ps[:, c, :], terms_t[:, c, :], ident_bf16[:])
+        terms = keep.tile([P, C], BF16)
+        nc.scalar.copy(out=terms[:], in_=terms_ps[:].rearrange("p c f -> p (c f)"))
+
+        def spread_over_batch(column):
+            bank = psum.tile([P, C], F32, tag="bank")
+            nc.tensor.matmul(
+                out=bank[:],
+                lhsT=pick[:, column : column + 1].to_broadcast([P, P]),
+                rhs=terms[:],
+                start=True,
+                stop=True,
+            )
+            return bank
+
+        gain = keep.tile([P, C], F32)
+        nc.scalar.copy(out=gain[:], in_=spread_over_batch(GAIN)[:])
 
         h_pairs = h_sb[:].rearrange("p l c -> p (l c)").bitcast(F32)
         pairs = C // 2
@@ -103,49 +162,6 @@ def tile_residualblock5_pb_e_kernel(tc, h, x, k2_words, k2_scales, b2, gamma2, b
                 in_=grouped[:, 2 * g * P * PACK : (2 * g + 2) * P * PACK],
             )
 
-        rows_t_ps = psum.tile([P, CHUNKS, P], BF16, tag="bank")
-        for c in range(CHUNKS):
-            nc.tensor.transpose(rows_t_ps[:, c, :], rows[:, c * P : (c + 1) * P], ident_bf16[:])
-        rows_t = keep.tile([P, CHUNKS, L + 4], F32)
-        nc.vector.tensor_copy(out=rows_t[:], in_=rows_t_ps[:, :, 0 : L + 4])
-        b2_t = rows_t[:, :, 0:L]
-        gamma_t = rows_t[:, :, L : L + 1]
-        beta_t = rows_t[:, :, L + 1 : L + 2]
-        mean_t = rows_t[:, :, L + 2 : L + 3]
-        var_t = rows_t[:, :, L + 3 : L + 4]
-
-        std_t = keep.tile([P, CHUNKS, 1], F32)
-        rstd_t = keep.tile([P, CHUNKS, 1], F32)
-        base_t = keep.tile([P, CHUNKS, 1], F32)
-        table_t = keep.tile([P, CHUNKS, L + 1], F32)
-        gain_t = table_t[:, :, GAIN : GAIN + 1]
-        shift_t = table_t[:, :, 0:L]
-        nc.vector.tensor_scalar_add(out=std_t[:], in0=var_t, scalar1=BN_EPS)
-        nc.scalar.sqrt(out=std_t[:], in_=std_t[:])
-        nc.vector.reciprocal(out=rstd_t[:], in_=std_t[:])
-        nc.vector.tensor_mul(out=gain_t, in0=gamma_t, in1=rstd_t[:])
-        nc.vector.tensor_mul(out=base_t[:], in0=mean_t, in1=gain_t)
-        nc.vector.tensor_sub(out=base_t[:], in0=beta_t, in1=base_t[:])
-        nc.vector.scalar_tensor_tensor(
-            out=shift_t, in0=b2_t, scalar=2.0, in1=gain_t.to_broadcast([P, CHUNKS, L]), op0=ALU.mult, op1=ALU.mult
-        )
-        nc.vector.tensor_add(out=shift_t, in0=shift_t, in1=base_t[:].to_broadcast([P, CHUNKS, L]))
-
-        def spread_over_batch(column):
-            bank = psum.tile([P, C], F32, tag="bank")
-            for c in range(CHUNKS):
-                nc.tensor.matmul(
-                    out=bank[:, c * P : (c + 1) * P],
-                    lhsT=table_t[:, c, column : column + 1].to_broadcast([P, P]),
-                    rhs=ident_f32[:],
-                    start=True,
-                    stop=True,
-                )
-            return bank
-
-        gain = keep.tile([P, C], F32)
-        nc.scalar.copy(out=gain[:], in_=spread_over_batch(GAIN)[:])
-
         addend = keep.tile([P, L, C], F32)
         result = keep.tile([P, L, C], F32)
 
@@ -174,7 +190,7 @@ def tile_residualblock5_pb_e_kernel(tc, h, x, k2_words, k2_scales, b2, gamma2, b
             nc.vector.scalar_tensor_tensor(
                 out=result[:, l, :], in0=z[:], scalar=LEAKY_ALPHA, in1=z[:], op0=ALU.mult, op1=ALU.max
             )
-            nc.scalar.dma_start(out=out[:, l, :], in_=result[:, l, :])
+            nc.sync.dma_start(out=out[:, l, :], in_=result[:, l, :])
 
         prepare_addend(0)
         for l in range(L):

@@ -192,8 +192,7 @@ def tile_residualblock5_pb_e_kernel(tc, h, x, k2_words, k2_scales, b2, gamma2, b
             )
             nc.sync.dma_start(out=out[:, l, :], in_=result[:, l, :])
 
-        prepare_addend(0)
         for l in range(L):
-            if l + 1 < L:
-                prepare_addend(l + 1)
+            prepare_addend(l)
+        for l in range(L):
             position(l)

@@ -39,6 +39,8 @@ def tile_residualblock5_pb_e_kernel(tc, h, x, k2_words, k2_scales, b2, gamma2, b
         work = ctx.enter_context(tc.tile_pool(name="work", bufs=3))
         psum = ctx.enter_context(tc.psum_pool(name="psum", bufs=8))
 
+        w_planes = keep.tile([P, SLOTS, C], U8, align_bytes=64)
+        nc.vector.memset(w_planes[:].rearrange("p s n -> p (s n)").bitcast(I32), 0)
         ident_f32 = keep.tile([P, P], F32)
         make_identity(nc, ident_f32[:])
         ident_bf16 = keep.tile([P, P], BF16)
@@ -49,8 +51,6 @@ def tile_residualblock5_pb_e_kernel(tc, h, x, k2_words, k2_scales, b2, gamma2, b
 
         rows = keep.tile([P, C], BF16)
         nc.vector.memset(rows[:], 0.0)
-        w_planes = keep.tile([P, SLOTS, C], U8, align_bytes=64)
-        nc.vector.memset(w_planes[:].rearrange("p s n -> p (s n)").bitcast(I32), 0)
         terms_t = keep.tile([P, CHUNKS, P], BF16)
         nc.vector.memset(terms_t[:], 0.0)
 
@@ -69,9 +69,9 @@ def tile_residualblock5_pb_e_kernel(tc, h, x, k2_words, k2_scales, b2, gamma2, b
         scales_by_row = k2_scales.rearrange("(s j) q n -> q j s n", j=OFFSETS)
         for q in range(SCALE_ROWS):
             first = 32 * (q // 4) + q % 4
-            nc.sync.dma_start(
-                out=w_planes[first : first + 4 * OFFSETS : 4, :, :].bitcast(I32),
-                in_=scales_by_row[q].bitcast(I32),
+            nc.gpsimd.dma_start(
+                out=w_planes[first : first + 4 * OFFSETS : 4, :, :].bitcast(F32),
+                in_=scales_by_row[q].bitcast(F32),
             )
 
         nc.sync.dma_start(out=x_sb[:], in_=x)

@@ -67,19 +67,33 @@ def tile_residualblock5_pb_e_kernel(tc, h, x, k2_words, k2_scales, b2, gamma2, b
         nc.sync.dma_start(out=h_sb[:, half_l:L, :], in_=h[:, half_l:L, :])
 
         scales_by_row = k2_scales.rearrange("(s j) q n -> q j s n", j=OFFSETS)
-        for q in range(SCALE_ROWS):
+
+        def load_scale_row(queue, q, view):
             first = 32 * (q // 4) + q % 4
-            nc.gpsimd.dma_start(
-                out=w_planes[first : first + 4 * OFFSETS : 4, :, :].bitcast(F32),
-                in_=scales_by_row[q].bitcast(F32),
+            queue.dma_start(
+                out=w_planes[first : first + 4 * OFFSETS : 4, :, :].bitcast(view),
+                in_=scales_by_row[q].bitcast(view),
             )
 
-        nc.sync.dma_start(out=x_sb[:], in_=x)
+        for q in range(SCALE_ROWS // 2, SCALE_ROWS):
+            load_scale_row(nc.gpsimd, q, F32)
 
         words_by_matrix = k2_words.rearrange("e p n t -> e p (n t)").bitcast(I32)
-        for l in range(L):
-            for i in range(TAPS):
-                nc.sync.dma_start(out=w_words[:, l, i, :].bitcast(I32), in_=words_by_matrix[L * i + l])
+
+        def load_x():
+            nc.sync.dma_start(out=x_sb[:], in_=x)
+
+        def load_matrix(l, i):
+            nc.sync.dma_start(out=w_words[:, l, i, :].bitcast(I32), in_=words_by_matrix[L * i + l])
+
+        big_loads = [(load_x, ())] + [(load_matrix, (l, i)) for l in range(L) for i in range(TAPS)]
+
+        sync_rows = list(range(SCALE_ROWS // 2))
+        for load, args in big_loads:
+            for q in sync_rows[0:2]:
+                load_scale_row(nc.sync, q, I32)
+            sync_rows = sync_rows[2:]
+            load(*args)
 
         rows_t_ps = psum.tile([P, CHUNKS, P], BF16, tag="bank")
         for c in range(CHUNKS):

@@ -28,6 +28,7 @@ VECTORS = L + 4
 GAIN = L
 TABLE = L + 1
 TERMS = 3
+SYNC_ONLY_POSITIONS = 2
 
 FLOPS = 2 * P * L * TAPS * C * C
 
@@ -38,6 +39,7 @@ def tile_residualblock5_pb_e_kernel(tc, h, x, k2_words, k2_scales, b2, gamma2, b
         keep = ctx.enter_context(tc.tile_pool(name="keep", bufs=1))
         work = ctx.enter_context(tc.tile_pool(name="work", bufs=3))
         psum = ctx.enter_context(tc.psum_pool(name="psum", bufs=8))
+        ctx.enter_context(tc.manual_schedule(engines={mybir.EngineType.SP, mybir.EngineType.Activation}))
 
         w_planes = keep.tile([P, SLOTS, C], U8, align_bytes=64)
         nc.vector.memset(w_planes[:].rearrange("p s n -> p (s n)").bitcast(I32), 0)
@@ -78,15 +80,17 @@ def tile_residualblock5_pb_e_kernel(tc, h, x, k2_words, k2_scales, b2, gamma2, b
         for q in range(SCALE_ROWS // 2, SCALE_ROWS):
             load_scale_row(nc.gpsimd, q, F32)
 
-        words_by_matrix = k2_words.rearrange("e p n t -> e p (n t)").bitcast(I32)
+        words_by_matrix = k2_words.rearrange("e p n t -> e p (n t)")
 
         def load_x():
             nc.sync.dma_start(out=x_sb[:], in_=x)
 
-        def load_matrix(l, i):
-            nc.sync.dma_start(out=w_words[:, l, i, :].bitcast(I32), in_=words_by_matrix[L * i + l])
+        def load_matrix(queue, view, l, i):
+            queue.dma_start(out=w_words[:, l, i, :].bitcast(view), in_=words_by_matrix[L * i + l].bitcast(view))
 
-        big_loads = [(load_x, ())] + [(load_matrix, (l, i)) for l in range(L) for i in range(TAPS)]
+        big_loads = [(load_x, ())] + [
+            (load_matrix, (nc.sync, I32, l, i)) for l in range(SYNC_ONLY_POSITIONS) for i in range(TAPS)
+        ]
 
         sync_rows = list(range(SCALE_ROWS // 2))
         for load, args in big_loads:
@@ -175,6 +179,13 @@ def tile_residualblock5_pb_e_kernel(tc, h, x, k2_words, k2_scales, b2, gamma2, b
                 scales=h_plane[:, cols],
                 in_=grouped[:, 2 * g * P * PACK : (2 * g + 2) * P * PACK],
             )
+
+        for l in range(SYNC_ONLY_POSITIONS, L):
+            for i in range(TAPS):
+                if (TAPS * l + i) % 2 == 0:
+                    load_matrix(nc.sync, I32, l, i)
+                else:
+                    load_matrix(nc.scalar, F32, l, i)
 
         addend = keep.tile([P, L, C], F32)
         result = keep.tile([P, L, C], F32)

@@ -136,7 +136,7 @@ def tile_residualblock5_pb_e_kernel(tc, h, x, k2_words, k2_scales, b2, gamma2, b
         for c in range(CHUNKS):
             nc.tensor.transpose(terms_ps[:, c, :], terms_t[:, c, :], ident_bf16[:])
         terms = keep.tile([P, C], BF16)
-        nc.scalar.copy(out=terms[:], in_=terms_ps[:].rearrange("p c f -> p (c f)"))
+        nc.vector.tensor_copy(out=terms[:], in_=terms_ps[:].rearrange("p c f -> p (c f)"))
 
         def spread_over_batch(column):
             bank = psum.tile([P, C], F32, tag="bank")
@@ -150,7 +150,7 @@ def tile_residualblock5_pb_e_kernel(tc, h, x, k2_words, k2_scales, b2, gamma2, b
             return bank
 
         gain = keep.tile([P, C], F32)
-        nc.scalar.copy(out=gain[:], in_=spread_over_batch(GAIN)[:])
+        nc.vector.tensor_copy(out=gain[:], in_=spread_over_batch(GAIN)[:])
 
         h_pairs = h_sb[:].rearrange("p l c -> p (l c)").bitcast(F32)
         pairs = C // 2
@@ -168,8 +168,7 @@ def tile_residualblock5_pb_e_kernel(tc, h, x, k2_words, k2_scales, b2, gamma2, b
                     nc.tensor.transpose(
                         flipped[:, l2, u, :], h_pairs[:, first + u : first + pairs : 2], ident_f32[:]
                     )
-            copy_out = nc.vector.tensor_copy if g % 2 == 0 else nc.scalar.copy
-            copy_out(
+            nc.vector.tensor_copy(
                 out=grouped_pairs[:, 2 * g : 2 * g + 2, :, :], in_=flipped[:].rearrange("p l u b -> p l b u")
             )
         for g in range(banks_of_h):
@@ -182,7 +181,7 @@ def tile_residualblock5_pb_e_kernel(tc, h, x, k2_words, k2_scales, b2, gamma2, b
 
         for l in range(SYNC_ONLY_POSITIONS, L):
             for i in range(TAPS):
-                if (TAPS * l + i) % 2 == 0:
+                if (TAPS * l + i) % 2 == 0 or l == L - 1:
                     load_matrix(nc.sync, I32, l, i)
                 else:
                     load_matrix(nc.scalar, F32, l, i)

@@ -27,6 +27,7 @@ CHUNKS = C // P
 VECTORS = L + 4
 GAIN = L
 TABLE = L + 1
+DMA_ALIGN = 256
 TERMS = 3
 SYNC_ONLY_POSITIONS = 2
 
@@ -41,7 +42,7 @@ def tile_residualblock5_pb_e_kernel(tc, h, x, k2_words, k2_scales, b2, gamma2, b
         psum = ctx.enter_context(tc.psum_pool(name="psum", bufs=8))
         ctx.enter_context(tc.manual_schedule(engines={mybir.EngineType.SP, mybir.EngineType.Activation}))
 
-        w_planes = keep.tile([P, SLOTS, C], U8, align_bytes=64)
+        w_planes = keep.tile([P, SLOTS, C], U8, align_bytes=DMA_ALIGN)
         nc.vector.memset(w_planes[:].rearrange("p s n -> p (s n)").bitcast(I32), 0)
         ident_f32 = keep.tile([P, P], F32)
         make_identity(nc, ident_f32[:])
@@ -60,9 +61,9 @@ def tile_residualblock5_pb_e_kernel(tc, h, x, k2_words, k2_scales, b2, gamma2, b
         for r, vec in enumerate((gamma2, beta2, mean2, var2)):
             nc.scalar.dma_start(out=rows[L + r : L + r + 1, :], in_=vec.rearrange("(o f) -> o f", o=1))
 
-        h_sb = keep.tile([P, L, C], BF16)
-        x_sb = keep.tile([P, L, C], BF16)
-        w_words = keep.tile([P, L, TAPS, C], U32, align_bytes=64)
+        h_sb = keep.tile([P, L, C], BF16, align_bytes=DMA_ALIGN)
+        x_sb = keep.tile([P, L, C], BF16, align_bytes=DMA_ALIGN)
+        w_words = keep.tile([P, L, TAPS, C], U32, align_bytes=DMA_ALIGN)
 
         half_l = L // 2
         nc.sync.dma_start(out=h_sb[:, 0:half_l, :], in_=h[:, 0:half_l, :])
@@ -187,7 +188,7 @@ def tile_residualblock5_pb_e_kernel(tc, h, x, k2_words, k2_scales, b2, gamma2, b
                     load_matrix(nc.scalar, F32, l, i)
 
         addend = keep.tile([P, L, C], F32)
-        result = keep.tile([P, L, C], F32)
+        result = keep.tile([P, L, C], F32, align_bytes=DMA_ALIGN)
 
         def prepare_addend(l):
             nc.vector.tensor_tensor(

@@ -28,6 +28,7 @@ VECTORS = L + 4
 GAIN = L
 TABLE = L + 1
 DMA_ALIGN = 256
+STORE_AFTER = {1: 0, 3: 2, 5: 4, 6: 6, 7: 7}
 TERMS = 3
 SYNC_ONLY_POSITIONS = 2
 
@@ -44,6 +45,8 @@ def tile_residualblock5_pb_e_kernel(tc, h, x, k2_words, k2_scales, b2, gamma2, b
 
         w_planes = keep.tile([P, SLOTS, C], U8, align_bytes=DMA_ALIGN)
         nc.vector.memset(w_planes[:].rearrange("p s n -> p (s n)").bitcast(I32), 0)
+        rows = keep.tile([P, C], BF16, align_bytes=DMA_ALIGN)
+        nc.gpsimd.memset(rows[:].bitcast(F32), 0.0)
         ident_f32 = keep.tile([P, P], F32)
         make_identity(nc, ident_f32[:])
         ident_bf16 = keep.tile([P, P], BF16)
@@ -52,8 +55,6 @@ def tile_residualblock5_pb_e_kernel(tc, h, x, k2_words, k2_scales, b2, gamma2, b
         nc.vector.tensor_add(out=pick[:], in0=ident_bf16[:, 0:TABLE], in1=ident_bf16[:, TABLE : 2 * TABLE])
         nc.vector.tensor_add(out=pick[:], in0=pick[:], in1=ident_bf16[:, 2 * TABLE : 3 * TABLE])
 
-        rows = keep.tile([P, C], BF16)
-        nc.vector.memset(rows[:], 0.0)
         terms_t = keep.tile([P, CHUNKS, P], BF16)
         nc.vector.memset(terms_t[:], 0.0)
 
@@ -215,7 +216,9 @@ def tile_residualblock5_pb_e_kernel(tc, h, x, k2_words, k2_scales, b2, gamma2, b
             nc.vector.scalar_tensor_tensor(
                 out=result[:, l, :], in0=z[:], scalar=LEAKY_ALPHA, in1=z[:], op0=ALU.mult, op1=ALU.max
             )
-            nc.sync.dma_start(out=out[:, l, :], in_=result[:, l, :])
+            if l in STORE_AFTER:
+                group = slice(STORE_AFTER[l], l + 1)
+                nc.sync.dma_start(out=out[:, group, :], in_=result[:, group, :])
 
         for l in range(L):
             prepare_addend(l)

@@ -27,7 +27,7 @@ CHUNKS = C // P
 VECTORS = L + 4
 GAIN = L
 TABLE = L + 1
-DMA_ALIGN = 256
+DMA_ALIGN = 2048
 STORE_AFTER = {1: 0, 3: 2, 5: 4, 6: 6, 7: 7}
 TERMS = 3
 SYNC_ONLY_POSITIONS = 2

@@ -28,7 +28,6 @@ VECTORS = L + 4
 GAIN = L
 TABLE = L + 1
 DMA_ALIGN = 2048
-STORE_AFTER = {1: 0, 3: 2, 5: 4, 6: 6, 7: 7}
 TERMS = 3
 SYNC_ONLY_POSITIONS = 2
 
@@ -39,7 +38,7 @@ def tile_residualblock5_pb_e_kernel(tc, h, x, k2_words, k2_scales, b2, gamma2, b
     nc = tc.nc
     with ExitStack() as ctx:
         keep = ctx.enter_context(tc.tile_pool(name="keep", bufs=1))
-        work = ctx.enter_context(tc.tile_pool(name="work", bufs=3))
+        work = ctx.enter_context(tc.tile_pool(name="work", bufs=4))
         psum = ctx.enter_context(tc.psum_pool(name="psum", bufs=8))
         ctx.enter_context(tc.manual_schedule(engines={mybir.EngineType.SP, mybir.EngineType.Activation}))
 
@@ -196,7 +195,7 @@ def tile_residualblock5_pb_e_kernel(tc, h, x, k2_words, k2_scales, b2, gamma2, b
                 out=addend[:, l, :], in0=spread_over_batch(l)[:], in1=x_sb[:, l, :], op=ALU.add
             )
 
-        def position(l):
+        def products(l):
             j, half = l % OFFSETS, l // OFFSETS
             y = psum.tile([P, C], F32, tag="bank")
             for i in range(TAPS):
@@ -210,17 +209,28 @@ def tile_residualblock5_pb_e_kernel(tc, h, x, k2_words, k2_scales, b2, gamma2, b
                     start=(i == 0),
                     stop=(i == TAPS - 1),
                 )
-            z = work.tile([P, C], F32)
-            nc.vector.tensor_tensor(out=z[:], in0=y[:], in1=gain[:], op=ALU.mult)
-            nc.vector.tensor_tensor(out=z[:], in0=z[:], in1=addend[:, l, :], op=ALU.add)
-            nc.vector.scalar_tensor_tensor(
-                out=result[:, l, :], in0=z[:], scalar=LEAKY_ALPHA, in1=z[:], op0=ALU.mult, op1=ALU.max
-            )
-            if l in STORE_AFTER:
-                group = slice(STORE_AFTER[l], l + 1)
-                nc.sync.dma_start(out=out[:, group, :], in_=result[:, group, :])
+            return y
+
+        def finish(positions, columns):
+            pieces = []
+            for l in positions:
+                y = products(l)
+                z = work.tile([P, C], F32)
+                pieces.extend([(l, cols, y, z) for cols in columns])
+            for l, cols, y, z in pieces:
+                nc.vector.tensor_tensor(out=z[:, cols], in0=y[:, cols], in1=gain[:, cols], op=ALU.mult)
+            for l, cols, y, z in pieces:
+                nc.vector.tensor_tensor(out=z[:, cols], in0=z[:, cols], in1=addend[:, l, cols], op=ALU.add)
+            for l, cols, y, z in pieces:
+                nc.vector.scalar_tensor_tensor(
+                    out=result[:, l, cols], in0=z[:, cols], scalar=LEAKY_ALPHA, in1=z[:, cols], op0=ALU.mult, op1=ALU.max
+                )
+            group = slice(positions[0], positions[-1] + 1)
+            nc.sync.dma_start(out=out[:, group, :], in_=result[:, group, :])
 
         for l in range(L):
             prepare_addend(l)
-        for l in range(L):
-            position(l)
+        for l in range(0, L - 2, 2):
+            finish((l, l + 1), (slice(0, C),))
+        for l in range(L - 2, L):
+            finish((l,), (slice(0, C // 2), slice(C // 2, C)))

@@ -40,7 +40,7 @@ def tile_residualblock5_pb_e_kernel(tc, h, x, k2_words, k2_scales, b2, gamma2, b
         keep = ctx.enter_context(tc.tile_pool(name="keep", bufs=1))
         work = ctx.enter_context(tc.tile_pool(name="work", bufs=4))
         psum = ctx.enter_context(tc.psum_pool(name="psum", bufs=8))
-        ctx.enter_context(tc.manual_schedule(engines={mybir.EngineType.SP, mybir.EngineType.Activation}))
+        ctx.enter_context(tc.manual_schedule(engines={mybir.EngineType.SP, mybir.EngineType.Activation, mybir.EngineType.PE}))
 
         w_planes = keep.tile([P, SLOTS, C], U8, align_bytes=DMA_ALIGN)
         nc.vector.memset(w_planes[:].rearrange("p s n -> p (s n)").bitcast(I32), 0)
@@ -105,6 +105,33 @@ def tile_residualblock5_pb_e_kernel(tc, h, x, k2_words, k2_scales, b2, gamma2, b
             nc.tensor.transpose(rows_t_ps[:, c, :], rows[:, c * P : (c + 1) * P], ident_bf16[:])
         rows_t = keep.tile([P, CHUNKS, VECTORS], F32)
         nc.vector.tensor_copy(out=rows_t[:], in_=rows_t_ps[:, :, 0:VECTORS])
+        h_pairs = h_sb[:].rearrange("p l c -> p (l c)").bitcast(F32)
+        pairs = C // 2
+        grouped = keep.tile([P, L * P * PACK], BF16, align_bytes=64)
+        grouped_pairs = grouped[:].bitcast(F32).rearrange("p (l b u) -> p l b u", l=L, u=2)
+        h_codes = keep.tile([P, L * P], U32, align_bytes=64)
+        h_plane = keep.tile([P, L * P], U8, align_bytes=64)
+
+        banks_of_h = L // 2
+        for g in range(banks_of_h):
+            flipped = psum.tile([P, 2, 2, P], F32, tag="bank")
+            for l2 in range(2):
+                for u in range(2):
+                    first = (2 * g + l2) * pairs
+                    nc.tensor.transpose(
+                        flipped[:, l2, u, :], h_pairs[:, first + u : first + pairs : 2], ident_f32[:]
+                    )
+            nc.vector.tensor_copy(
+                out=grouped_pairs[:, 2 * g : 2 * g + 2, :, :], in_=flipped[:].rearrange("p l u b -> p l b u")
+            )
+        for g in range(banks_of_h):
+            cols = slice(2 * g * P, (2 * g + 2) * P)
+            nc.vector.quantize_mx(
+                out=h_codes[:, cols].bitcast(FP8X4),
+                scales=h_plane[:, cols],
+                in_=grouped[:, 2 * g * P * PACK : (2 * g + 2) * P * PACK],
+            )
+
         b2_t = rows_t[:, :, 0:L]
         gamma_t = rows_t[:, :, L : L + 1]
         beta_t = rows_t[:, :, L + 1 : L + 2]
@@ -153,33 +180,6 @@ def tile_residualblock5_pb_e_kernel(tc, h, x, k2_words, k2_scales, b2, gamma2, b
         gain = keep.tile([P, C], F32)
         nc.vector.tensor_copy(out=gain[:], in_=spread_over_batch(GAIN)[:])
 
-        h_pairs = h_sb[:].rearrange("p l c -> p (l c)").bitcast(F32)
-        pairs = C // 2
-        grouped = keep.tile([P, L * P * PACK], BF16, align_bytes=64)
-        grouped_pairs = grouped[:].bitcast(F32).rearrange("p (l b u) -> p l b u", l=L, u=2)
-        h_codes = keep.tile([P, L * P], U32, align_bytes=64)
-        h_plane = keep.tile([P, L * P], U8, align_bytes=64)
-
-        banks_of_h = L // 2
-        for g in range(banks_of_h):
-            flipped = psum.tile([P, 2, 2, P], F32, tag="bank")
-            for l2 in range(2):
-                for u in range(2):
-                    first = (2 * g + l2) * pairs
-                    nc.tensor.transpose(
-                        flipped[:, l2, u, :], h_pairs[:, first + u : first + pairs : 2], ident_f32[:]
-                    )
-            nc.vector.tensor_copy(
-                out=grouped_pairs[:, 2 * g : 2 * g + 2, :, :], in_=flipped[:].rearrange("p l u b -> p l b u")
-            )
-        for g in range(banks_of_h):
-            cols = slice(2 * g * P, (2 * g + 2) * P)
-            nc.vector.quantize_mx(
-                out=h_codes[:, cols].bitcast(FP8X4),
-                scales=h_plane[:, cols],
-                in_=grouped[:, 2 * g * P * PACK : (2 * g + 2) * P * PACK],
-            )
-
         for l in range(SYNC_ONLY_POSITIONS, L):
             for i in range(TAPS):
                 if (TAPS * l + i) % 2 == 0 or l == L - 1:
@@ -211,7 +211,7 @@ def tile_residualblock5_pb_e_kernel(tc, h, x, k2_words, k2_scales, b2, gamma2, b
                 )
             return y
 
-        def finish(positions, columns):
+        def finish(positions, columns, store_columns):
             pieces = []
             for l in positions:
                 y = products(l)
@@ -226,11 +226,13 @@ def tile_residualblock5_pb_e_kernel(tc, h, x, k2_words, k2_scales, b2, gamma2, b
                     out=result[:, l, cols], in0=z[:, cols], scalar=LEAKY_ALPHA, in1=z[:, cols], op0=ALU.mult, op1=ALU.max
                 )
             group = slice(positions[0], positions[-1] + 1)
-            nc.sync.dma_start(out=out[:, group, :], in_=result[:, group, :])
+            for cols in store_columns:
+                nc.sync.dma_start(out=out[:, group, cols], in_=result[:, group, cols])
 
         for l in range(L):
             prepare_addend(l)
+        whole, halves = (slice(0, C),), (slice(0, C // 2), slice(C // 2, C))
         for l in range(0, L - 2, 2):
-            finish((l, l + 1), (slice(0, C),))
-        for l in range(L - 2, L):
-            finish((l,), (slice(0, C // 2), slice(C // 2, C)))
+            finish((l, l + 1), whole, whole)
+        finish((L - 2,), halves, whole)
+        finish((L - 1,), halves, halves)

from contextlib import ExitStack

import concourse.mybir as mybir
from concourse.masks import make_identity

F32 = mybir.dt.float32
BF16 = mybir.dt.bfloat16
I32 = mybir.dt.int32
U32 = mybir.dt.uint32
U8 = mybir.dt.uint8
FP8X4 = mybir.dt.float8_e4m3fn_x4
ALU = mybir.AluOpType

P = 128
L = 8
C = 512
TAPS = 5
TAP_STEP = (0, 0, 1, -1, 2)
BN_EPS = 1e-3
LEAKY_ALPHA = 0.3

PACK = 4
SCALE_ROWS = C // 32
OFFSETS = 4
SLOTS = TAPS * L // OFFSETS
CHUNKS = C // P
VECTORS = L + 4
GAIN = L
TABLE = L + 1
DMA_ALIGN = 2048
TERMS = 3
SYNC_ONLY_POSITIONS = 2

FLOPS = 2 * P * L * TAPS * C * C


def tile_residualblock5_pb_e_kernel(tc, h, x, k2_words, k2_scales, b2, gamma2, beta2, mean2, var2, out):
    nc = tc.nc
    with ExitStack() as ctx:
        keep = ctx.enter_context(tc.tile_pool(name="keep", bufs=1))
        work = ctx.enter_context(tc.tile_pool(name="work", bufs=4))
        psum = ctx.enter_context(tc.psum_pool(name="psum", bufs=8))
        ctx.enter_context(tc.manual_schedule(engines={mybir.EngineType.SP, mybir.EngineType.Activation, mybir.EngineType.PE}))

        w_planes = keep.tile([P, SLOTS, C], U8, align_bytes=DMA_ALIGN)
        nc.vector.memset(w_planes[:].rearrange("p s n -> p (s n)").bitcast(I32), 0)
        rows = keep.tile([P, C], BF16, align_bytes=DMA_ALIGN)
        nc.gpsimd.memset(rows[:].bitcast(F32), 0.0)
        ident_f32 = keep.tile([P, P], F32)
        make_identity(nc, ident_f32[:])
        ident_bf16 = keep.tile([P, P], BF16)
        nc.vector.tensor_copy(out=ident_bf16[:], in_=ident_f32[:])
        pick = keep.tile([P, TABLE], BF16)
        nc.vector.tensor_add(out=pick[:], in0=ident_bf16[:, 0:TABLE], in1=ident_bf16[:, TABLE : 2 * TABLE])
        nc.vector.tensor_add(out=pick[:], in0=pick[:], in1=ident_bf16[:, 2 * TABLE : 3 * TABLE])

        terms_t = keep.tile([P, CHUNKS, P], BF16)
        nc.vector.memset(terms_t[:], 0.0)

        nc.scalar.dma_start(out=rows[0:L, :], in_=b2)
        for r, vec in enumerate((gamma2, beta2, mean2, var2)):
            nc.scalar.dma_start(out=rows[L + r : L + r + 1, :], in_=vec.rearrange("(o f) -> o f", o=1))

        h_sb = keep.tile([P, L, C], BF16, align_bytes=DMA_ALIGN)
        x_sb = keep.tile([P, L, C], BF16, align_bytes=DMA_ALIGN)
        w_words = keep.tile([P, L, TAPS, C], U32, align_bytes=DMA_ALIGN)

        half_l = L // 2
        nc.sync.dma_start(out=h_sb[:, 0:half_l, :], in_=h[:, 0:half_l, :])
        nc.sync.dma_start(out=h_sb[:, half_l:L, :], in_=h[:, half_l:L, :])

        scales_by_row = k2_scales.rearrange("(s j) q n -> q j s n", j=OFFSETS)

        def load_scale_row(queue, q, view):
            first = 32 * (q // 4) + q % 4
            queue.dma_start(
                out=w_planes[first : first + 4 * OFFSETS : 4, :, :].bitcast(view),
                in_=scales_by_row[q].bitcast(view),
            )

        for q in range(SCALE_ROWS // 2, SCALE_ROWS):
            load_scale_row(nc.gpsimd, q, F32)

        words_by_matrix = k2_words.rearrange("e p n t -> e p (n t)")

        def load_x():
            nc.sync.dma_start(out=x_sb[:], in_=x)

        def load_matrix(queue, view, l, i):
            queue.dma_start(out=w_words[:, l, i, :].bitcast(view), in_=words_by_matrix[L * i + l].bitcast(view))

        big_loads = [(load_x, ())] + [
            (load_matrix, (nc.sync, I32, l, i)) for l in range(SYNC_ONLY_POSITIONS) for i in range(TAPS)
        ]

        sync_rows = list(range(SCALE_ROWS // 2))
        for load, args in big_loads:
            for q in sync_rows[0:2]:
                load_scale_row(nc.sync, q, I32)
            sync_rows = sync_rows[2:]
            load(*args)

        rows_t_ps = psum.tile([P, CHUNKS, P], BF16, tag="bank")
        for c in range(CHUNKS):
            nc.tensor.transpose(rows_t_ps[:, c, :], rows[:, c * P : (c + 1) * P], ident_bf16[:])
        rows_t = keep.tile([P, CHUNKS, VECTORS], F32)
        nc.vector.tensor_copy(out=rows_t[:], in_=rows_t_ps[:, :, 0:VECTORS])
        h_pairs = h_sb[:].rearrange("p l c -> p (l c)").bitcast(F32)
        pairs = C // 2
        grouped = keep.tile([P, L * P * PACK], BF16, align_bytes=64)
        grouped_pairs = grouped[:].bitcast(F32).rearrange("p (l b u) -> p l b u", l=L, u=2)
        h_codes = keep.tile([P, L * P], U32, align_bytes=64)
        h_plane = keep.tile([P, L * P], U8, align_bytes=64)

        banks_of_h = L // 2
        for g in range(banks_of_h):
            flipped = psum.tile([P, 2, 2, P], F32, tag="bank")
            for l2 in range(2):
                for u in range(2):
                    first = (2 * g + l2) * pairs
                    nc.tensor.transpose(
                        flipped[:, l2, u, :], h_pairs[:, first + u : first + pairs : 2], ident_f32[:]
                    )
            nc.vector.tensor_copy(
                out=grouped_pairs[:, 2 * g : 2 * g + 2, :, :], in_=flipped[:].rearrange("p l u b -> p l b u")
            )
        for g in range(banks_of_h):
            cols = slice(2 * g * P, (2 * g + 2) * P)
            nc.vector.quantize_mx(
                out=h_codes[:, cols].bitcast(FP8X4),
                scales=h_plane[:, cols],
                in_=grouped[:, 2 * g * P * PACK : (2 * g + 2) * P * PACK],
            )

        b2_t = rows_t[:, :, 0:L]
        gamma_t = rows_t[:, :, L : L + 1]
        beta_t = rows_t[:, :, L + 1 : L + 2]
        mean_t = rows_t[:, :, L + 2 : L + 3]
        var_t = rows_t[:, :, L + 3 : L + 4]

        std_t = keep.tile([P, CHUNKS, 1], F32)
        rstd_t = keep.tile([P, CHUNKS, 1], F32)
        base_t = keep.tile([P, CHUNKS, 1], F32)
        table_t = keep.tile([P, CHUNKS, TABLE], F32)
        gain_t = table_t[:, :, GAIN : GAIN + 1]
        shift_t = table_t[:, :, 0:L]
        nc.vector.tensor_scalar_add(out=std_t[:], in0=var_t, scalar1=BN_EPS)
        nc.scalar.sqrt(out=std_t[:], in_=std_t[:])
        nc.vector.reciprocal(out=rstd_t[:], in_=std_t[:])
        nc.vector.tensor_mul(out=gain_t, in0=gamma_t, in1=rstd_t[:])
        nc.vector.tensor_mul(out=base_t[:], in0=mean_t, in1=gain_t)
        nc.vector.tensor_sub(out=base_t[:], in0=beta_t, in1=base_t[:])
        nc.vector.scalar_tensor_tensor(
            out=shift_t, in0=b2_t, scalar=2.0, in1=gain_t.to_broadcast([P, CHUNKS, L]), op0=ALU.mult, op1=ALU.mult
        )
        nc.vector.tensor_add(out=shift_t, in0=shift_t, in1=base_t[:].to_broadcast([P, CHUNKS, L]))

        for s in range(TERMS):
            term = terms_t[:, :, TABLE * s : TABLE * (s + 1)]
            nc.vector.tensor_copy(out=term, in_=table_t[:])
            if s + 1 < TERMS:
                nc.vector.tensor_sub(out=table_t[:], in0=table_t[:], in1=term)
        terms_ps = psum.tile([P, CHUNKS, P], BF16, tag="bank")
        for c in range(CHUNKS):
            nc.tensor.transpose(terms_ps[:, c, :], terms_t[:, c, :], ident_bf16[:])
        terms = keep.tile([P, C], BF16)
        nc.vector.tensor_copy(out=terms[:], in_=terms_ps[:].rearrange("p c f -> p (c f)"))

        def spread_over_batch(column):
            bank = psum.tile([P, C], F32, tag="bank")
            nc.tensor.matmul(
                out=bank[:],
                lhsT=pick[:, column : column + 1].to_broadcast([P, P]),
                rhs=terms[:],
                start=True,
                stop=True,
            )
            return bank

        gain = keep.tile([P, C], F32)
        nc.vector.tensor_copy(out=gain[:], in_=spread_over_batch(GAIN)[:])

        for l in range(SYNC_ONLY_POSITIONS, L):
            for i in range(TAPS):
                if (TAPS * l + i) % 2 == 0 or l == L - 1:
                    load_matrix(nc.sync, I32, l, i)
                else:
                    load_matrix(nc.scalar, F32, l, i)

        addend = keep.tile([P, L, C], F32)
        result = keep.tile([P, L, C], F32, align_bytes=DMA_ALIGN)

        def prepare_addend(l):
            nc.vector.tensor_tensor(
                out=addend[:, l, :], in0=spread_over_batch(l)[:], in1=x_sb[:, l, :], op=ALU.add
            )

        def products(l):
            j, half = l % OFFSETS, l // OFFSETS
            y = psum.tile([P, C], F32, tag="bank")
            for i in range(TAPS):
                source = (l - TAP_STEP[i]) % L
                nc.tensor.matmul_mx(
                    out=y[:],
                    lhsT=h_codes[:, source * P : (source + 1) * P].bitcast(FP8X4),
                    lhsT_scale=h_plane[:, source * P : (source + 1) * P],
                    rhs=w_words[:, l, i, :].bitcast(FP8X4),
                    rhs_scale=w_planes[4 * j : P, 2 * i + half, :],
                    start=(i == 0),
                    stop=(i == TAPS - 1),
                )
            return y

        def finish(positions, columns, store_columns):
            pieces = []
            for l in positions:
                y = products(l)
                z = work.tile([P, C], F32)
                pieces.extend([(l, cols, y, z) for cols in columns])
            for l, cols, y, z in pieces:
                nc.vector.tensor_tensor(out=z[:, cols], in0=y[:, cols], in1=gain[:, cols], op=ALU.mult)
            for l, cols, y, z in pieces:
                nc.vector.tensor_tensor(out=z[:, cols], in0=z[:, cols], in1=addend[:, l, cols], op=ALU.add)
            for l, cols, y, z in pieces:
                nc.vector.scalar_tensor_tensor(
                    out=result[:, l, cols], in0=z[:, cols], scalar=LEAKY_ALPHA, in1=z[:, cols], op0=ALU.mult, op1=ALU.max
                )
            group = slice(positions[0], positions[-1] + 1)
            for cols in store_columns:
                nc.sync.dma_start(out=out[:, group, cols], in_=result[:, group, cols])

        for l in range(L):
            prepare_addend(l)
        whole, halves = (slice(0, C),), (slice(0, C // 2), slice(C // 2, C))
        for l in range(0, L - 2, 2):
            finish((l, l + 1), whole, whole)
        finish((L - 2,), halves, whole)
        finish((L - 1,), halves, halves)
